import numpy as np
import ml_dtypes


def mxq(x, axis, fmt="e4m3"):
    dtype, down = {"e4m3": (ml_dtypes.float8_e4m3fn, 7), "e5m2": (ml_dtypes.float8_e5m2, 14)}[fmt]
    v = np.moveaxis(np.asarray(x, np.float32).astype(ml_dtypes.bfloat16).astype(np.float64), axis, -1)
    blocks = v.reshape(v.shape[:-1] + (-1, 32))
    amax = np.abs(blocks).max(-1, keepdims=True)
    byte = np.maximum(np.where(amax > 0, np.frexp(amax)[1] - 1 + 127, 0) - down, 1)
    scale = np.exp2(byte - 127.0)
    codes = (blocks / scale).astype(np.float32).astype(dtype).astype(np.float64)
    return np.moveaxis((codes * scale).reshape(v.shape), -1, axis)


WIDE = False


def mx_kscale(k):
    if not WIDE:
        return np.ones(k)
    levels = np.array([10, -10, 5, -5, 0])
    a = np.random.permutation(np.resize(levels, k // 512 * 4)).reshape(k // 512, 4)
    idx = np.arange(k)
    return np.exp2(a[idx // 512, idx % 128 // 32])


BF16 = ml_dtypes.bfloat16


def bf(x):
    return np.asarray(x, np.float32).astype(BF16)


def f64(x):
    return np.asarray(x).astype(np.float64)


E2M1 = np.array([0.0, 0.5, 1.0, 1.5, 2.0, 3.0, 4.0, 6.0, -0.0, -0.5, -1.0, -1.5, -2.0, -3.0, -4.0, -6.0])


def pack_weight(w, fmt):
    k, n = w.shape
    w = f64(bf(w)).reshape(k // 32, 32, n)
    amax = np.abs(w).max(1)
    if fmt == "e4m3":
        byte = np.frexp(amax)[1] - 1 + 127 - 7
    else:
        mant, ex = np.frexp(amax / 6.0)
        byte = np.where(mant > 0.5, ex, ex - 1) + 127
    byte = np.clip(np.where(amax > 0, byte, 1), 1, 254)
    scaled = (w * np.exp2(127.0 - byte)[:, None, :]).reshape(k, n).astype(np.float32)
    by_word = np.ascontiguousarray(scaled.reshape(k // 512, 128, 4, n).transpose(0, 1, 3, 2))
    if fmt == "e4m3":
        words = by_word.astype(ml_dtypes.float8_e4m3fn).view(np.uint8)
    else:
        c = by_word.astype(ml_dtypes.float4_e2m1fn).view(np.uint8) & 0xF
        words = c[..., 0::2] | (c[..., 1::2] << 4)
    return np.ascontiguousarray(words), np.ascontiguousarray(byte.astype(np.uint8).reshape(k // 512, 16, n))


def unpack_weight(words, scales, fmt):
    g, p, n, _ = words.shape
    if fmt == "e4m3":
        vals = np.ascontiguousarray(words).view(ml_dtypes.float8_e4m3fn).astype(np.float64)
    else:
        nib = np.empty((g, p, n, 4), np.uint8)
        nib[..., 0::2] = words & 0xF
        nib[..., 1::2] = words >> 4
        vals = E2M1[nib]
    vals = vals * np.repeat(np.exp2(scales.astype(np.float64) - 127.0), 8, axis=1)[..., None]
    return vals.transpose(0, 1, 3, 2).reshape(g * 512, n)


B, S, H, NH, NKV, HD = 2, 64, 3072, 32, 16, 128
ROPE_THETA = 10000.0
FMT = "e4m3"


def rope_tables():
    inv_freq = 1.0 / (ROPE_THETA ** (np.arange(0, HD, 2) / HD))
    pos = np.arange(S)[None, :] + np.random.randint(0, S, (B, 1))
    freqs = pos[:, :, None] * inv_freq[None, None, :]
    emb = np.concatenate([freqs, freqs], axis=-1)
    return np.cos(emb), np.sin(emb)


def rotate_half(x):
    x1, x2 = np.split(x, 2, axis=-1)
    return np.concatenate([-x2, x1], axis=-1)


def setup_inputs():
    s = mx_kscale(H)
    hidden_states = bf(np.random.standard_normal((B, S, H)) * s)
    q_w = np.random.standard_normal((NH * HD, H)) / np.sqrt(H) / s[None, :]
    k_w = np.random.standard_normal((NKV * HD, H)) / np.sqrt(H) / s[None, :]
    v_w = np.random.standard_normal((NKV * HD, H)) / np.sqrt(H) / s[None, :]
    q_w_words, q_w_scales = pack_weight(np.ascontiguousarray(q_w.T), FMT)
    k_w_words, k_w_scales = pack_weight(np.ascontiguousarray(k_w.T), FMT)
    v_w_words, v_w_scales = pack_weight(np.ascontiguousarray(v_w.T), FMT)
    cos, sin = rope_tables()
    return {"hidden_states": hidden_states, "cos": bf(cos), "sin": bf(sin), "q_w_words": q_w_words, "q_w_scales": q_w_scales, "k_w_words": k_w_words, "k_w_scales": k_w_scales, "v_w_words": v_w_words, "v_w_scales": v_w_scales}


def reference(hidden_states, cos, sin, q_w_words, q_w_scales, k_w_words, k_w_scales, v_w_words, v_w_scales):
    b, s, _ = hidden_states.shape
    xq = mxq(f64(hidden_states), 2, "e4m3")
    q = (xq @ unpack_weight(q_w_words, q_w_scales, FMT)).reshape(b, s, NH, HD).transpose(0, 2, 1, 3)
    k = (xq @ unpack_weight(k_w_words, k_w_scales, FMT)).reshape(b, s, NKV, HD).transpose(0, 2, 1, 3)
    v = (xq @ unpack_weight(v_w_words, v_w_scales, FMT)).reshape(b, s, NKV, HD).transpose(0, 2, 1, 3)
    c = f64(cos)[:, None, :, :]
    sn = f64(sin)[:, None, :, :]
    q = q * c + rotate_half(q) * sn
    k = k * c + rotate_half(k) * sn
    return (q, k, v)

@@ -1,0 +1,189 @@
+from contextlib import ExitStack
+
+import concourse.bass as bass
+import concourse.mybir as mybir
+import concourse.tile as tile
+from concourse.masks import make_identity
+
+F32 = mybir.dt.float32
+BF16 = mybir.dt.bfloat16
+I32 = mybir.dt.int32
+U32 = mybir.dt.uint32
+U8 = mybir.dt.uint8
+FP8X4 = mybir.dt.float8_e4m3fn_x4
+MULT = mybir.AluOpType.mult
+ADD = mybir.AluOpType.add
+
+P = 128
+B, S, H, HD = 2, 64, 3072, 128
+G = H // 512
+NQ, NKV = 4096, 2048
+BANK = 512
+ROUND = 2048
+FLOPS = 2 * B * S * H * (NQ + 2 * NKV)
+
+
+def tile_mistralattention_w_kernel(
+    tc, hidden_states, cos, sin,
+    q_w_words, q_w_scales, k_w_words, k_w_scales, v_w_words, v_w_scales,
+    out_0, out_1, out_2,
+):
+    nc = tc.nc
+    with ExitStack() as ctx:
+        const = ctx.enter_context(tc.tile_pool(name="const", bufs=1))
+        wpool = ctx.enter_context(tc.tile_pool(name="wpool", bufs=18))
+        wlast = ctx.enter_context(tc.tile_pool(name="wlast", bufs=4))
+        rpool = ctx.enter_context(tc.tile_pool(name="rpool", bufs=4))
+        tpool = ctx.enter_context(tc.tile_pool(name="tpool", bufs=2))
+        psum = ctx.enter_context(tc.psum_pool(name="psum", bufs=8))
+
+        pa = const.tile([P, NQ + 2 * NKV], U8, align_bytes=64)
+        pb = const.tile([P, NQ], U8, align_bytes=64)
+        nc.vector.memset(pa[:, 0:NQ].bitcast(I32), 0)
+        nc.vector.memset(pb[:].bitcast(I32), 0)
+        nc.vector.memset(pa[:, NQ:NQ + 2 * NKV].bitcast(I32), 0)
+
+        x_sb = const.tile([P, H], BF16, align_bytes=64)
+        for b in range(B):
+            nc.sync.dma_start(out=x_sb[b:P:2, :], in_=hidden_states[b])
+        cos_bf = const.tile([P, HD], BF16)
+        sin_bf = const.tile([P, HD], BF16)
+        for b in range(B):
+            nc.scalar.dma_start(out=cos_bf[b:P:2, :], in_=cos[b])
+            nc.scalar.dma_start(out=sin_bf[b:P:2, :], in_=sin[b])
+
+        ident = const.tile([P, P], F32)
+        make_identity(nc, ident[:])
+
+        specs = (
+            (q_w_scales, 0, NQ, 0, 0),
+            (k_w_scales, NQ, NKV, 8, 0),
+            (v_w_scales, NQ + NKV, NKV, 8, NKV),
+        )
+        for scl, ca, n, off_b, cb in specs:
+            for quad in (0, 2, 1, 3):
+                nc.sync.dma_start(
+                    out=pa[32 * quad:32 * quad + 16, ca:ca + n].bitcast(I32),
+                    in_=scl[0:4, 4 * quad:4 * quad + 4, :].bitcast(I32),
+                )
+            for quad in (0, 2, 1, 3):
+                nc.sync.dma_start(
+                    out=pb[32 * quad + off_b:32 * quad + off_b + 8, cb:cb + n].bitcast(I32),
+                    in_=scl[4:6, 4 * quad:4 * quad + 4, :].bitcast(I32),
+                )
+
+        cos_f = const.tile([P, HD], F32)
+        swp_f = const.tile([P, HD], F32)
+        nc.vector.tensor_copy(out=cos_f[:], in_=cos_bf[:])
+        nc.vector.tensor_copy(out=swp_f[:, 0:64], in_=sin_bf[:, 64:128])
+        nc.vector.tensor_scalar(out=swp_f[:, 64:128], in0=sin_bf[:, 0:64], scalar1=-1.0, scalar2=None, op0=MULT)
+
+        xw = x_sb[:].bitcast(F32)
+        grouped = const.tile([P, G, P, 4], BF16, align_bytes=64)
+        grouped_w = grouped[:].bitcast(F32)
+        x_codes = const.tile([P, G * P], U32, align_bytes=64)
+        x_scales = const.tile([P, G * P], U8, align_bytes=64)
+        xts = []
+        for j in range(G // 2):
+            xt = psum.tile([P, 2, 2, P], F32, tag="bank", name="xt%d" % j)
+            for gi in range(2):
+                g = 2 * j + gi
+                for u in range(2):
+                    nc.tensor.transpose(xt[:, gi, u, :], xw[:, 256 * g + u:256 * (g + 1):2], ident[:])
+            xts.append(xt)
+        for j in range(G // 2):
+            src = xts[j][:].rearrange("p g u m -> p g m u")
+            dst = grouped_w[:, 2 * j:2 * j + 2, :, :]
+            if j == 1:
+                nc.scalar.copy(out=dst, in_=src)
+            else:
+                nc.vector.tensor_copy(out=dst, in_=src)
+        for j in range(G // 2):
+            nc.vector.quantize_mx(
+                out=x_codes[:, 256 * j:256 * (j + 1)].bitcast(FP8X4),
+                scales=x_scales[:, 256 * j:256 * (j + 1)],
+                in_=grouped[:, 2 * j:2 * j + 2, :, :].rearrange("p g m t -> p (g m t)"),
+            )
+
+        def plane(kind, g, c0, n):
+            scl, ca, width, off_b, cb = specs[kind]
+            if g < 4:
+                return pa[4 * g:P, ca + c0:ca + c0 + n]
+            off = off_b + 4 * (g - 4)
+            return pb[off:P, cb + c0:cb + c0 + n]
+
+        def passes(accs, kind, g, c0, wt, banks):
+            for j in banks:
+                lo = BANK * j if wt.shape[1] == ROUND else 0
+                nc.tensor.matmul_mx(
+                    out=accs[j][:],
+                    lhsT=x_codes[:, P * g:P * (g + 1)].bitcast(FP8X4),
+                    lhsT_scale=x_scales[:, P * g:P * (g + 1)],
+                    rhs=wt[:, lo:lo + BANK].bitcast(FP8X4),
+                    rhs_scale=plane(kind, g, c0 + BANK * j, BANK),
+                    start=(g == 0),
+                    stop=(g == G - 1),
+                )
+
+        rounds = (
+            (0, q_w_words, 0, out_0, 0),
+            (0, q_w_words, ROUND, out_0, 16),
+            (1, k_w_words, 0, out_1, 0),
+            (2, v_w_words, 0, out_2, 0),
+        )
+        for kind, words, c0, out, h0 in rounds:
+            accs = [psum.tile([P, BANK], F32, tag="bank", name="acc%d_%d_%d" % (kind, c0, j)) for j in range(4)]
+            for g in range(G):
+                flat = words[g].rearrange("p n t -> p (n t)")
+                if kind == 2 and g == G - 1:
+                    for j in range(4):
+                        wl = wlast.tile([P, BANK], U32, align_bytes=64, tag="wl", name="wl%d" % j)
+                        nc.sync.dma_start(
+                            out=wl[:].bitcast(I32),
+                            in_=flat[:, 4 * BANK * j:4 * BANK * (j + 1)].bitcast(I32),
+                        )
+                        passes(accs, kind, g, c0, wl, (j,))
+                else:
+                    wt = wpool.tile([P, ROUND], U32, align_bytes=64, tag="wt", name="wt%d_%d_%d" % (kind, c0, g))
+                    nc.sync.dma_start(
+                        out=wt[:].bitcast(I32),
+                        in_=flat[:, 4 * c0:4 * (c0 + ROUND)].bitcast(I32),
+                    )
+                    passes(accs, kind, g, c0, wt, range(4))
+
+            if kind < 2:
+                for half in range(2):
+                    res = rpool.tile([P, 2 * BANK], F32, tag="res", name="res%d_%d_%d" % (kind, c0, half))
+                    tmp = tpool.tile([P, 2 * BANK], F32, tag="tmp", name="tmp%d_%d_%d" % (kind, c0, half))
+                    for jj in range(2):
+                        acc = accs[2 * half + jj][:].rearrange("p (h d) -> p h d", d=HD)
+                        cols = slice(BANK * jj, BANK * (jj + 1))
+                        nc.vector.tensor_tensor(
+                            out=res[:, cols].rearrange("p (h d) -> p h d", d=HD), in0=acc,
+                            in1=cos_f[:].unsqueeze(1).to_broadcast([P, 4, HD]), op=MULT)
+                        nc.vector.tensor_tensor(
+                            out=tmp[:, cols].rearrange("p (h d) -> p h d", d=HD), in0=acc,
+                            in1=swp_f[:].unsqueeze(1).to_broadcast([P, 4, HD]), op=MULT)
+                    res4 = res[:].rearrange("p (h w d) -> p h w d", w=2, d=64)
+                    tmp4 = tmp[:].rearrange("p (h w d) -> p h w d", w=2, d=64)
+                    for w in range(2):
+                        nc.vector.tensor_tensor(out=res4[:, :, w, :], in0=res4[:, :, w, :], in1=tmp4[:, :, 1 - w, :], op=ADD)
+                    hh = h0 + 8 * half
+                    for b in range(B):
+                        nc.gpsimd.dma_start(
+                            out=out[b, hh:hh + 8].rearrange("h s d -> s h d"),
+                            in_=res[b:P:2, :].rearrange("p (h d) -> p h d", d=HD),
+                        )
+            else:
+                for j in range(4):
+                    vres = rpool.tile([P, BANK], F32, tag="vres", name="vres%d" % j)
+                    if j % 2 == 0:
+                        nc.vector.tensor_copy(out=vres[:], in_=accs[j][:])
+                    else:
+                        nc.scalar.copy(out=vres[:], in_=accs[j][:])
+                    for b in range(B):
+                        eng = nc.sync if b == 0 else nc.scalar
+                        eng.dma_start(
+                            out=out[b, 4 * j:4 * j + 4].rearrange("h s d -> s h d"),
+                            in_=vres[b:P:2, :].rearrange("p (h d) -> p h d", d=HD),
+                        )

@@ -62,14 +62,14 @@ def tile_mistralattention_w_kernel(
         )
         for scl, ca, n, off_b, cb in specs:
             for quad in (0, 2, 1, 3):
-                nc.sync.dma_start(
-                    out=pa[32 * quad:32 * quad + 16, ca:ca + n].bitcast(I32),
-                    in_=scl[0:4, 4 * quad:4 * quad + 4, :].bitcast(I32),
+                nc.gpsimd.dma_start(
+                    out=pa[32 * quad:32 * quad + 16, ca:ca + n].bitcast(F32),
+                    in_=scl[0:4, 4 * quad:4 * quad + 4, :].bitcast(F32),
                 )
             for quad in (0, 2, 1, 3):
-                nc.sync.dma_start(
-                    out=pb[32 * quad + off_b:32 * quad + off_b + 8, cb:cb + n].bitcast(I32),
-                    in_=scl[4:6, 4 * quad:4 * quad + 4, :].bitcast(I32),
+                nc.gpsimd.dma_start(
+                    out=pb[32 * quad + off_b:32 * quad + off_b + 8, cb:cb + n].bitcast(F32),
+                    in_=scl[4:6, 4 * quad:4 * quad + 4, :].bitcast(F32),
                 )
 
         cos_f = const.tile([P, HD], F32)

@@ -170,7 +170,7 @@ def tile_mistralattention_w_kernel(
                         nc.vector.tensor_tensor(out=res4[:, :, w, :], in0=res4[:, :, w, :], in1=tmp4[:, :, 1 - w, :], op=ADD)
                     hh = h0 + 8 * half
                     for b in range(B):
-                        nc.gpsimd.dma_start(
+                        nc.scalar.dma_start(
                             out=out[b, hh:hh + 8].rearrange("h s d -> s h d"),
                             in_=res[b:P:2, :].rearrange("p (h d) -> p h d", d=HD),
                         )

@@ -1,8 +1,6 @@
 from contextlib import ExitStack
 
-import concourse.bass as bass
 import concourse.mybir as mybir
-import concourse.tile as tile
 from concourse.masks import make_identity
 
 F32 = mybir.dt.float32
@@ -20,6 +18,7 @@ G = H // 512
 NQ, NKV = 4096, 2048
 BANK = 512
 ROUND = 2048
+SP, SI = 4, 16
 FLOPS = 2 * B * S * H * (NQ + 2 * NKV)
 
 
@@ -31,11 +30,16 @@ def tile_mistralattention_w_kernel(
     nc = tc.nc
     with ExitStack() as ctx:
         const = ctx.enter_context(tc.tile_pool(name="const", bufs=1))
-        wpool = ctx.enter_context(tc.tile_pool(name="wpool", bufs=18))
+        wpool = ctx.enter_context(tc.tile_pool(name="wpool", bufs=14))
         wlast = ctx.enter_context(tc.tile_pool(name="wlast", bufs=4))
-        rpool = ctx.enter_context(tc.tile_pool(name="rpool", bufs=4))
+        zpool = ctx.enter_context(tc.tile_pool(name="zpool", bufs=2))
+        rpool = ctx.enter_context(tc.tile_pool(name="rpool", bufs=2))
         tpool = ctx.enter_context(tc.tile_pool(name="tpool", bufs=2))
+        vpool = ctx.enter_context(tc.tile_pool(name="vpool", bufs=4))
         psum = ctx.enter_context(tc.psum_pool(name="psum", bufs=8))
+
+        def bank(name):
+            return psum.tile([P, BANK], F32, tag="bank", name=name)
 
         pa = const.tile([P, NQ + 2 * NKV], U8, align_bytes=64)
         pb = const.tile([P, NQ], U8, align_bytes=64)
@@ -44,13 +48,15 @@ def tile_mistralattention_w_kernel(
         nc.vector.memset(pa[:, NQ:NQ + 2 * NKV].bitcast(I32), 0)
 
         x_sb = const.tile([P, H], BF16, align_bytes=64)
+        nc.sync.dma_start(out=x_sb[:], in_=hidden_states.rearrange("b s k -> (b s) k"))
+
+        cosr = zpool.tile([P, SI * HD], BF16, tag="zt", name="cosr")
+        sinr = zpool.tile([P, SI * HD], BF16, tag="zt", name="sinr")
+        nc.vector.memset(cosr[:].bitcast(I32), 0)
+        nc.vector.memset(sinr[:].bitcast(I32), 0)
         for b in range(B):
-            nc.sync.dma_start(out=x_sb[b:P:2, :], in_=hidden_states[b])
-        cos_bf = const.tile([P, HD], BF16)
-        sin_bf = const.tile([P, HD], BF16)
-        for b in range(B):
-            nc.scalar.dma_start(out=cos_bf[b:P:2, :], in_=cos[b])
-            nc.scalar.dma_start(out=sin_bf[b:P:2, :], in_=sin[b])
+            nc.scalar.dma_start(out=cosr[b:2 * SP:2, :], in_=cos[b].rearrange("(sp si) d -> sp (si d)", sp=SP))
+            nc.scalar.dma_start(out=sinr[b:2 * SP:2, :], in_=sin[b].rearrange("(sp si) d -> sp (si d)", sp=SP))
 
         ident = const.tile([P, P], F32)
         make_identity(nc, ident[:])
@@ -72,38 +78,68 @@ def tile_mistralattention_w_kernel(
                     in_=scl[4:6, 4 * quad:4 * quad + 4, :].bitcast(F32),
                 )
 
-        cos_f = const.tile([P, HD], F32)
-        swp_f = const.tile([P, HD], F32)
-        nc.vector.tensor_copy(out=cos_f[:], in_=cos_bf[:])
-        nc.vector.tensor_copy(out=swp_f[:, 0:64], in_=sin_bf[:, 64:128])
-        nc.vector.tensor_scalar(out=swp_f[:, 64:128], in0=sin_bf[:, 0:64], scalar1=-1.0, scalar2=None, op0=MULT)
+        perm_v = const.tile([P, P], F32)
+        perm_t = const.tile([P, P], F32)
+        nc.vector.tensor_copy(
+            out=perm_v[:].rearrange("p (s b) -> p s b", b=B),
+            in_=ident[:].rearrange("p (b s) -> p s b", b=B))
+        nc.vector.tensor_copy(
+            out=perm_t[:].rearrange("p (sp b si) -> p sp b si", sp=SP, b=B),
+            in_=ident[:].rearrange("p (b sp si) -> p sp b si", sp=SP, b=B))
+        sel = const.tile([P, P], BF16)
+        nc.vector.tensor_copy(
+            out=sel[:].rearrange("p (h e) -> p h e", e=8),
+            in_=ident[:, 0:8].unsqueeze(1).to_broadcast([P, 16, 8]))
 
         xw = x_sb[:].bitcast(F32)
-        grouped = const.tile([P, G, P, 4], BF16, align_bytes=64)
-        grouped_w = grouped[:].bitcast(F32)
-        x_codes = const.tile([P, G * P], U32, align_bytes=64)
-        x_scales = const.tile([P, G * P], U8, align_bytes=64)
-        xts = []
-        for j in range(G // 2):
-            xt = psum.tile([P, 2, 2, P], F32, tag="bank", name="xt%d" % j)
-            for gi in range(2):
-                g = 2 * j + gi
-                for u in range(2):
-                    nc.tensor.transpose(xt[:, gi, u, :], xw[:, 256 * g + u:256 * (g + 1):2], ident[:])
-            xts.append(xt)
-        for j in range(G // 2):
-            src = xts[j][:].rearrange("p g u m -> p g m u")
-            dst = grouped_w[:, 2 * j:2 * j + 2, :, :]
-            if j == 1:
-                nc.scalar.copy(out=dst, in_=src)
-            else:
-                nc.vector.tensor_copy(out=dst, in_=src)
-        for j in range(G // 2):
-            nc.vector.quantize_mx(
-                out=x_codes[:, 256 * j:256 * (j + 1)].bitcast(FP8X4),
-                scales=x_scales[:, 256 * j:256 * (j + 1)],
-                in_=grouped[:, 2 * j:2 * j + 2, :, :].rearrange("p g m t -> p (g m t)"),
-            )
+        codes = []
+        for which, perm in ((0, perm_t), (1, perm_v)):
+            grouped = const.tile([P, G, P, 4], BF16, align_bytes=64, name="grouped%d" % which)
+            grouped_w = grouped[:].bitcast(F32)
+            x_codes = const.tile([P, G * P], U32, align_bytes=64, name="x_codes%d" % which)
+            x_scales = const.tile([P, G * P], U8, align_bytes=64, name="x_scales%d" % which)
+            xts = []
+            for j in range(G // 2):
+                xt = bank("xt%d_%d" % (which, j))
+                for gi in range(2):
+                    g = 2 * j + gi
+                    for u in range(2):
+                        nc.tensor.transpose(
+                            xt[:, 128 * (2 * gi + u):128 * (2 * gi + u + 1)],
+                            xw[:, 256 * g + u:256 * (g + 1):2], perm[:])
+                xts.append(xt)
+            for j in range(G // 2):
+                src = xts[j][:].rearrange("p (g u m) -> p g m u", g=2, u=2)
+                dst = grouped_w[:, 2 * j:2 * j + 2, :, :]
+                if j == 1:
+                    nc.scalar.copy(out=dst, in_=src)
+                else:
+                    nc.vector.tensor_copy(out=dst, in_=src)
+            for j in range(G // 2):
+                nc.vector.quantize_mx(
+                    out=x_codes[:, 256 * j:256 * (j + 1)].bitcast(FP8X4),
+                    scales=x_scales[:, 256 * j:256 * (j + 1)],
+                    in_=grouped[:, 2 * j:2 * j + 2, :, :].rearrange("p g m t -> p (g m t)"),
+                )
+            codes.append((x_codes, x_scales))
+        xt_codes, xt_scales = codes[0]
+        xv_codes, xv_scales = codes[1]
+
+        ssr = rpool.tile([P, SI * HD], BF16, tag="res", name="ssr")
+        sin3 = sinr[:].rearrange("p (si w d) -> p si w d", w=2, d=64)
+        ssr3 = ssr[:].rearrange("p (si w d) -> p si w d", w=2, d=64)
+        nc.vector.tensor_copy(out=ssr3[:, :, 0, :], in_=sin3[:, :, 1, :])
+        nc.vector.tensor_scalar(out=ssr3[:, :, 1, :], in0=sin3[:, :, 0, :], scalar1=-1.0, scalar2=None, op0=MULT)
+        cos_t = const.tile([P, SI * HD], F32)
+        swp_t = const.tile([P, SI * HD], F32)
+        for which, (rows, table) in enumerate(((cosr, cos_t), (ssr, swp_t))):
+            for c in range(4):
+                tb = bank("tb%d_%d" % (which, c))
+                nc.tensor.matmul(out=tb[:], lhsT=sel[:], rhs=rows[:, BANK * c:BANK * (c + 1)], start=True, stop=True)
+                if c % 2 == 0:
+                    nc.scalar.copy(out=table[:, BANK * c:BANK * (c + 1)], in_=tb[:])
+                else:
+                    nc.vector.tensor_copy(out=table[:, BANK * c:BANK * (c + 1)], in_=tb[:])
 
         def plane(kind, g, c0, n):
             scl, ca, width, off_b, cb = specs[kind]
@@ -112,78 +148,98 @@ def tile_mistralattention_w_kernel(
             off = off_b + 4 * (g - 4)
             return pb[off:P, cb + c0:cb + c0 + n]
 
-        def passes(accs, kind, g, c0, wt, banks):
-            for j in banks:
-                lo = BANK * j if wt.shape[1] == ROUND else 0
+        def load(kind, words, c0, g):
+            wt = wpool.tile([P, ROUND], U32, align_bytes=64, tag="wt", name="wt%d_%d_%d" % (kind, c0, g))
+            flat = words[g].rearrange("p n t -> p (n t)")
+            nc.sync.dma_start(out=wt[:].bitcast(I32), in_=flat[:, 4 * c0:4 * (c0 + ROUND)].bitcast(I32))
+            return wt
+
+        def rotary_round(kind, words, c0, out, h0, cuts):
+            label = "%d_%d" % (kind, c0)
+            wts = [load(kind, words, c0, g) for g in range(G)]
+            yts = [bank("yt%s_%d" % (label, bk)) for bk in range(4)]
+
+            def one_pass(bk, slot, g):
+                col = HD * (4 * bk + slot)
                 nc.tensor.matmul_mx(
-                    out=accs[j][:],
-                    lhsT=x_codes[:, P * g:P * (g + 1)].bitcast(FP8X4),
-                    lhsT_scale=x_scales[:, P * g:P * (g + 1)],
-                    rhs=wt[:, lo:lo + BANK].bitcast(FP8X4),
-                    rhs_scale=plane(kind, g, c0 + BANK * j, BANK),
+                    out=yts[bk][:, HD * slot:HD * (slot + 1)],
+                    lhsT=wts[g][:, col:col + HD].bitcast(FP8X4),
+                    lhsT_scale=plane(kind, g, c0 + col, HD),
+                    rhs=xt_codes[:, P * g:P * (g + 1)].bitcast(FP8X4),
+                    rhs_scale=xt_scales[:, P * g:P * (g + 1)],
                     start=(g == 0),
                     stop=(g == G - 1),
                 )
 
-        rounds = (
-            (0, q_w_words, 0, out_0, 0),
-            (0, q_w_words, ROUND, out_0, 16),
-            (1, k_w_words, 0, out_1, 0),
-            (2, v_w_words, 0, out_2, 0),
-        )
-        for kind, words, c0, out, h0 in rounds:
-            accs = [psum.tile([P, BANK], F32, tag="bank", name="acc%d_%d_%d" % (kind, c0, j)) for j in range(4)]
             for g in range(G):
-                flat = words[g].rearrange("p n t -> p (n t)")
-                if kind == 2 and g == G - 1:
-                    for j in range(4):
-                        wl = wlast.tile([P, BANK], U32, align_bytes=64, tag="wl", name="wl%d" % j)
-                        nc.sync.dma_start(
-                            out=wl[:].bitcast(I32),
-                            in_=flat[:, 4 * BANK * j:4 * BANK * (j + 1)].bitcast(I32),
+                for bk in range(4):
+                    one_pass(bk, 0, g)
+            zt = zpool.tile([P, SI, P], F32, tag="zt", name="zt%s" % label)
+            for bk in range(4):
+                for slot in range(1, 4):
+                    for g in range(G):
+                        one_pass(bk, slot, g)
+                nc.scalar.copy(
+                    out=zt[:, :, 32 * bk:32 * (bk + 1)],
+                    in_=yts[bk][:].rearrange("p (he si) -> p si he", si=SI))
+            fs = [bank("f%s_%d" % (label, c)) for c in range(4)]
+            for si in range(SI):
+                nc.tensor.transpose(fs[si // 4][:, HD * (si % 4):HD * (si % 4 + 1)], zt[:, si, :], ident[:])
+            res = rpool.tile([P, ROUND], F32, tag="res", name="res%s" % label)
+            for half in range(2):
+                tmp = tpool.tile([P, 2 * BANK], F32, tag="tmp", name="tmp%s_%d" % (label, half))
+                for jj in range(2):
+                    c = 2 * half + jj
+                    cols = slice(BANK * c, BANK * (c + 1))
+                    nc.vector.tensor_tensor(out=res[:, cols], in0=fs[c][:], in1=cos_t[:, cols], op=MULT)
+                    nc.vector.tensor_tensor(out=tmp[:, BANK * jj:BANK * (jj + 1)], in0=fs[c][:], in1=swp_t[:, cols], op=MULT)
+                res4 = res[:, 2 * BANK * half:2 * BANK * (half + 1)].rearrange("p (n w d) -> p n w d", w=2, d=64)
+                tmp4 = tmp[:].rearrange("p (n w d) -> p n w d", w=2, d=64)
+                for w in range(2):
+                    nc.vector.tensor_tensor(out=res4[:, :, w, :], in0=res4[:, :, w, :], in1=tmp4[:, :, 1 - w, :], op=ADD)
+                if cuts == 2 or half == 1:
+                    lo = 2 * BANK * half if cuts == 2 else 0
+                    for b in range(B):
+                        nc.gpsimd.dma_start(
+                            out=out[b, h0:h0 + 16].rearrange("h (sp si) d -> (h sp) (si d)", sp=SP)[:, lo:2 * BANK * (half + 1)],
+                            in_=res[b:P:2, lo:2 * BANK * (half + 1)],
                         )
-                        passes(accs, kind, g, c0, wl, (j,))
-                else:
-                    wt = wpool.tile([P, ROUND], U32, align_bytes=64, tag="wt", name="wt%d_%d_%d" % (kind, c0, g))
-                    nc.sync.dma_start(
-                        out=wt[:].bitcast(I32),
-                        in_=flat[:, 4 * c0:4 * (c0 + ROUND)].bitcast(I32),
-                    )
-                    passes(accs, kind, g, c0, wt, range(4))
 
-            if kind < 2:
-                for half in range(2):
-                    res = rpool.tile([P, 2 * BANK], F32, tag="res", name="res%d_%d_%d" % (kind, c0, half))
-                    tmp = tpool.tile([P, 2 * BANK], F32, tag="tmp", name="tmp%d_%d_%d" % (kind, c0, half))
-                    for jj in range(2):
-                        acc = accs[2 * half + jj][:].rearrange("p (h d) -> p h d", d=HD)
-                        cols = slice(BANK * jj, BANK * (jj + 1))
-                        nc.vector.tensor_tensor(
-                            out=res[:, cols].rearrange("p (h d) -> p h d", d=HD), in0=acc,
-                            in1=cos_f[:].unsqueeze(1).to_broadcast([P, 4, HD]), op=MULT)
-                        nc.vector.tensor_tensor(
-                            out=tmp[:, cols].rearrange("p (h d) -> p h d", d=HD), in0=acc,
-                            in1=swp_f[:].unsqueeze(1).to_broadcast([P, 4, HD]), op=MULT)
-                    res4 = res[:].rearrange("p (h w d) -> p h w d", w=2, d=64)
-                    tmp4 = tmp[:].rearrange("p (h w d) -> p h w d", w=2, d=64)
-                    for w in range(2):
-                        nc.vector.tensor_tensor(out=res4[:, :, w, :], in0=res4[:, :, w, :], in1=tmp4[:, :, 1 - w, :], op=ADD)
-                    hh = h0 + 8 * half
-                    for b in range(B):
-                        nc.scalar.dma_start(
-                            out=out[b, hh:hh + 8].rearrange("h s d -> s h d"),
-                            in_=res[b:P:2, :].rearrange("p (h d) -> p h d", d=HD),
-                        )
+        rotary_round(0, q_w_words, 0, out_0, 0, 1)
+        rotary_round(0, q_w_words, ROUND, out_0, 16, 1)
+        rotary_round(1, k_w_words, 0, out_1, 0, 2)
+
+        accs = [bank("acc%d" % j) for j in range(4)]
+
+        def v_pass(g, j, wt, lo):
+            nc.tensor.matmul_mx(
+                out=accs[j][:],
+                lhsT=xv_codes[:, P * g:P * (g + 1)].bitcast(FP8X4),
+                lhsT_scale=xv_scales[:, P * g:P * (g + 1)],
+                rhs=wt[:, lo:lo + BANK].bitcast(FP8X4),
+                rhs_scale=plane(2, g, BANK * j, BANK),
+                start=(g == 0),
+                stop=(g == G - 1),
+            )
+
+        for g in range(G - 1):
+            wt = load(2, v_w_words, 0, g)
+            for j in range(4):
+                v_pass(g, j, wt, BANK * j)
+        flat = v_w_words[G - 1].rearrange("p n t -> p (n t)")
+        for j in range(4):
+            wl = wlast.tile([P, BANK], U32, align_bytes=64, tag="wl", name="wl%d" % j)
+            nc.sync.dma_start(out=wl[:].bitcast(I32), in_=flat[:, 4 * BANK * j:4 * BANK * (j + 1)].bitcast(I32))
+            v_pass(G - 1, j, wl, 0)
+        for j in range(4):
+            vres = vpool.tile([P, BANK], F32, tag="vres", name="vres%d" % j)
+            if j % 2 == 0:
+                nc.vector.tensor_copy(out=vres[:], in_=accs[j][:])
             else:
-                for j in range(4):
-                    vres = rpool.tile([P, BANK], F32, tag="vres", name="vres%d" % j)
-                    if j % 2 == 0:
-                        nc.vector.tensor_copy(out=vres[:], in_=accs[j][:])
-                    else:
-                        nc.scalar.copy(out=vres[:], in_=accs[j][:])
-                    for b in range(B):
-                        eng = nc.sync if b == 0 else nc.scalar
-                        eng.dma_start(
-                            out=out[b, 4 * j:4 * j + 4].rearrange("h s d -> s h d"),
-                            in_=vres[b:P:2, :].rearrange("p (h d) -> p h d", d=HD),
-                        )
+                nc.scalar.copy(out=vres[:], in_=accs[j][:])
+            for b in range(B):
+                eng = nc.sync if b == 0 else nc.scalar
+                eng.dma_start(
+                    out=out_2[b, 4 * j:4 * j + 4].rearrange("h s d -> s h d"),
+                    in_=vres[b:P:2, :].rearrange("p (h d) -> p h d", d=HD),
+                )

@@ -19,6 +19,7 @@ NQ, NKV = 4096, 2048
 BANK = 512
 ROUND = 2048
 SP, SI = 4, 16
+PB_OFF = (0, 8, 8)
 FLOPS = 2 * B * S * H * (NQ + 2 * NKV)
 
 
@@ -30,22 +31,25 @@ def tile_mistralattention_w_kernel(
     nc = tc.nc
     with ExitStack() as ctx:
         const = ctx.enter_context(tc.tile_pool(name="const", bufs=1))
-        wpool = ctx.enter_context(tc.tile_pool(name="wpool", bufs=14))
-        wlast = ctx.enter_context(tc.tile_pool(name="wlast", bufs=4))
+        wpool = ctx.enter_context(tc.tile_pool(name="wpool", bufs=13))
+        wlast = ctx.enter_context(tc.tile_pool(name="wlast", bufs=8))
         zpool = ctx.enter_context(tc.tile_pool(name="zpool", bufs=2))
         rpool = ctx.enter_context(tc.tile_pool(name="rpool", bufs=2))
         tpool = ctx.enter_context(tc.tile_pool(name="tpool", bufs=2))
         vpool = ctx.enter_context(tc.tile_pool(name="vpool", bufs=4))
         psum = ctx.enter_context(tc.psum_pool(name="psum", bufs=8))
+        ctx.enter_context(tc.manual_schedule())
 
         def bank(name):
             return psum.tile([P, BANK], F32, tag="bank", name=name)
 
-        pa = const.tile([P, NQ + 2 * NKV], U8, align_bytes=64)
-        pb = const.tile([P, NQ], U8, align_bytes=64)
-        nc.vector.memset(pa[:, 0:NQ].bitcast(I32), 0)
-        nc.vector.memset(pb[:].bitcast(I32), 0)
-        nc.vector.memset(pa[:, NQ:NQ + 2 * NKV].bitcast(I32), 0)
+        planes = []
+        for kind, n in enumerate((NQ, NKV, NKV)):
+            pa = const.tile([P, n], U8, align_bytes=64, name="pa%d" % kind)
+            pb = const.tile([P, n], U8, align_bytes=64, name="pb%d" % kind)
+            nc.vector.memset(pa[:].bitcast(I32), 0)
+            nc.vector.memset(pb[:].bitcast(I32), 0)
+            planes.append((pa, pb))
 
         x_sb = const.tile([P, H], BF16, align_bytes=64)
         nc.sync.dma_start(out=x_sb[:], in_=hidden_states.rearrange("b s k -> (b s) k"))
@@ -61,20 +65,16 @@ def tile_mistralattention_w_kernel(
         ident = const.tile([P, P], F32)
         make_identity(nc, ident[:])
 
-        specs = (
-            (q_w_scales, 0, NQ, 0, 0),
-            (k_w_scales, NQ, NKV, 8, 0),
-            (v_w_scales, NQ + NKV, NKV, 8, NKV),
-        )
-        for scl, ca, n, off_b, cb in specs:
+        for kind, scl in enumerate((q_w_scales, k_w_scales, v_w_scales)):
+            pa, pb = planes[kind]
             for quad in (0, 2, 1, 3):
                 nc.gpsimd.dma_start(
-                    out=pa[32 * quad:32 * quad + 16, ca:ca + n].bitcast(F32),
+                    out=pa[32 * quad:32 * quad + 16, :].bitcast(F32),
                     in_=scl[0:4, 4 * quad:4 * quad + 4, :].bitcast(F32),
                 )
             for quad in (0, 2, 1, 3):
                 nc.gpsimd.dma_start(
-                    out=pb[32 * quad + off_b:32 * quad + off_b + 8, cb:cb + n].bitcast(F32),
+                    out=pb[32 * quad + PB_OFF[kind]:32 * quad + PB_OFF[kind] + 8, :].bitcast(F32),
                     in_=scl[4:6, 4 * quad:4 * quad + 4, :].bitcast(F32),
                 )
 
@@ -142,11 +142,10 @@ def tile_mistralattention_w_kernel(
                     nc.vector.tensor_copy(out=table[:, BANK * c:BANK * (c + 1)], in_=tb[:])
 
         def plane(kind, g, c0, n):
-            scl, ca, width, off_b, cb = specs[kind]
+            pa, pb = planes[kind]
             if g < 4:
-                return pa[4 * g:P, ca + c0:ca + c0 + n]
-            off = off_b + 4 * (g - 4)
-            return pb[off:P, cb + c0:cb + c0 + n]
+                return pa[4 * g:P, c0:c0 + n]
+            return pb[PB_OFF[kind] + 4 * (g - 4):P, c0:c0 + n]
 
         def load(kind, words, c0, g):
             wt = wpool.tile([P, ROUND], U32, align_bytes=64, tag="wt", name="wt%d_%d_%d" % (kind, c0, g))
@@ -222,24 +221,21 @@ def tile_mistralattention_w_kernel(
                 stop=(g == G - 1),
             )
 
-        for g in range(G - 1):
+        for g in range(G - 2):
             wt = load(2, v_w_words, 0, g)
             for j in range(4):
                 v_pass(g, j, wt, BANK * j)
-        flat = v_w_words[G - 1].rearrange("p n t -> p (n t)")
         for j in range(4):
-            wl = wlast.tile([P, BANK], U32, align_bytes=64, tag="wl", name="wl%d" % j)
-            nc.sync.dma_start(out=wl[:].bitcast(I32), in_=flat[:, 4 * BANK * j:4 * BANK * (j + 1)].bitcast(I32))
-            v_pass(G - 1, j, wl, 0)
+            for g in (G - 2, G - 1):
+                wl = wlast.tile([P, BANK], U32, align_bytes=64, tag="wl", name="wl%d_%d" % (g, j))
+                flat = v_w_words[g].rearrange("p n t -> p (n t)")
+                nc.sync.dma_start(out=wl[:].bitcast(I32), in_=flat[:, 4 * BANK * j:4 * BANK * (j + 1)].bitcast(I32))
+                v_pass(g, j, wl, 0)
         for j in range(4):
             vres = vpool.tile([P, BANK], F32, tag="vres", name="vres%d" % j)
-            if j % 2 == 0:
-                nc.vector.tensor_copy(out=vres[:], in_=accs[j][:])
-            else:
-                nc.scalar.copy(out=vres[:], in_=accs[j][:])
+            nc.scalar.copy(out=vres[:], in_=accs[j][:])
             for b in range(B):
-                eng = nc.sync if b == 0 else nc.scalar
-                eng.dma_start(
+                nc.sync.dma_start(
                     out=out_2[b, 4 * j:4 * j + 4].rearrange("h s d -> s h d"),
                     in_=vres[b:P:2, :].rearrange("p (h d) -> p h d", d=HD),
                 )

@@ -31,14 +31,13 @@ def tile_mistralattention_w_kernel(
     nc = tc.nc
     with ExitStack() as ctx:
         const = ctx.enter_context(tc.tile_pool(name="const", bufs=1))
-        wpool = ctx.enter_context(tc.tile_pool(name="wpool", bufs=13))
-        wlast = ctx.enter_context(tc.tile_pool(name="wlast", bufs=8))
+        wpool = ctx.enter_context(tc.tile_pool(name="wpool", bufs=14))
+        wlast = ctx.enter_context(tc.tile_pool(name="wlast", bufs=4))
         zpool = ctx.enter_context(tc.tile_pool(name="zpool", bufs=2))
         rpool = ctx.enter_context(tc.tile_pool(name="rpool", bufs=2))
         tpool = ctx.enter_context(tc.tile_pool(name="tpool", bufs=2))
         vpool = ctx.enter_context(tc.tile_pool(name="vpool", bufs=4))
         psum = ctx.enter_context(tc.psum_pool(name="psum", bufs=8))
-        ctx.enter_context(tc.manual_schedule())
 
         def bank(name):
             return psum.tile([P, BANK], F32, tag="bank", name=name)
@@ -221,21 +220,24 @@ def tile_mistralattention_w_kernel(
                 stop=(g == G - 1),
             )
 
-        for g in range(G - 2):
+        for g in range(G - 1):
             wt = load(2, v_w_words, 0, g)
             for j in range(4):
                 v_pass(g, j, wt, BANK * j)
+        flat = v_w_words[G - 1].rearrange("p n t -> p (n t)")
         for j in range(4):
-            for g in (G - 2, G - 1):
-                wl = wlast.tile([P, BANK], U32, align_bytes=64, tag="wl", name="wl%d_%d" % (g, j))
-                flat = v_w_words[g].rearrange("p n t -> p (n t)")
-                nc.sync.dma_start(out=wl[:].bitcast(I32), in_=flat[:, 4 * BANK * j:4 * BANK * (j + 1)].bitcast(I32))
-                v_pass(g, j, wl, 0)
+            wl = wlast.tile([P, BANK], U32, align_bytes=64, tag="wl", name="wl%d" % j)
+            nc.sync.dma_start(out=wl[:].bitcast(I32), in_=flat[:, 4 * BANK * j:4 * BANK * (j + 1)].bitcast(I32))
+            v_pass(G - 1, j, wl, 0)
         for j in range(4):
             vres = vpool.tile([P, BANK], F32, tag="vres", name="vres%d" % j)
-            nc.scalar.copy(out=vres[:], in_=accs[j][:])
+            if j % 2 == 0:
+                nc.vector.tensor_copy(out=vres[:], in_=accs[j][:])
+            else:
+                nc.scalar.copy(out=vres[:], in_=accs[j][:])
             for b in range(B):
-                nc.sync.dma_start(
+                eng = nc.sync if b == 0 else nc.scalar
+                eng.dma_start(
                     out=out_2[b, 4 * j:4 * j + 4].rearrange("h s d -> s h d"),
                     in_=vres[b:P:2, :].rearrange("p (h d) -> p h d", d=HD),
                 )

@@ -31,13 +31,14 @@ def tile_mistralattention_w_kernel(
     nc = tc.nc
     with ExitStack() as ctx:
         const = ctx.enter_context(tc.tile_pool(name="const", bufs=1))
-        wpool = ctx.enter_context(tc.tile_pool(name="wpool", bufs=14))
-        wlast = ctx.enter_context(tc.tile_pool(name="wlast", bufs=4))
+        wpool = ctx.enter_context(tc.tile_pool(name="wpool", bufs=13))
+        wlast = ctx.enter_context(tc.tile_pool(name="wlast", bufs=8))
         zpool = ctx.enter_context(tc.tile_pool(name="zpool", bufs=2))
         rpool = ctx.enter_context(tc.tile_pool(name="rpool", bufs=2))
         tpool = ctx.enter_context(tc.tile_pool(name="tpool", bufs=2))
         vpool = ctx.enter_context(tc.tile_pool(name="vpool", bufs=4))
         psum = ctx.enter_context(tc.psum_pool(name="psum", bufs=8))
+        ctx.enter_context(tc.manual_schedule())
 
         def bank(name):
             return psum.tile([P, BANK], F32, tag="bank", name=name)
@@ -60,6 +61,12 @@ def tile_mistralattention_w_kernel(
         for b in range(B):
             nc.scalar.dma_start(out=cosr[b:2 * SP:2, :], in_=cos[b].rearrange("(sp si) d -> sp (si d)", sp=SP))
             nc.scalar.dma_start(out=sinr[b:2 * SP:2, :], in_=sin[b].rearrange("(sp si) d -> sp (si d)", sp=SP))
+
+        cos_bf = const.tile([P, HD], BF16)
+        sin_bf = const.tile([P, HD], BF16)
+        for b in range(B):
+            nc.scalar.dma_start(out=cos_bf[b:P:2, :], in_=cos[b])
+            nc.scalar.dma_start(out=sin_bf[b:P:2, :], in_=sin[b])
 
         ident = const.tile([P, P], F32)
         make_identity(nc, ident[:])
@@ -140,6 +147,12 @@ def tile_mistralattention_w_kernel(
                 else:
                     nc.vector.tensor_copy(out=table[:, BANK * c:BANK * (c + 1)], in_=tb[:])
 
+        cos_f = const.tile([P, HD], F32)
+        swp_f = const.tile([P, HD], F32)
+        nc.vector.tensor_copy(out=cos_f[:], in_=cos_bf[:])
+        nc.vector.tensor_copy(out=swp_f[:, 0:64], in_=sin_bf[:, 64:128])
+        nc.vector.tensor_scalar(out=swp_f[:, 64:128], in0=sin_bf[:, 0:64], scalar1=-1.0, scalar2=None, op0=MULT)
+
         def plane(kind, g, c0, n):
             pa, pb = planes[kind]
             if g < 4:
@@ -205,39 +218,61 @@ def tile_mistralattention_w_kernel(
 
         rotary_round(0, q_w_words, 0, out_0, 0, 1)
         rotary_round(0, q_w_words, ROUND, out_0, 16, 1)
-        rotary_round(1, k_w_words, 0, out_1, 0, 2)
 
-        accs = [bank("acc%d" % j) for j in range(4)]
-
-        def v_pass(g, j, wt, lo):
+        def x_pass(accs, kind, g, j, wt, lo):
             nc.tensor.matmul_mx(
                 out=accs[j][:],
                 lhsT=xv_codes[:, P * g:P * (g + 1)].bitcast(FP8X4),
                 lhsT_scale=xv_scales[:, P * g:P * (g + 1)],
                 rhs=wt[:, lo:lo + BANK].bitcast(FP8X4),
-                rhs_scale=plane(2, g, BANK * j, BANK),
+                rhs_scale=plane(kind, g, BANK * j, BANK),
                 start=(g == 0),
                 stop=(g == G - 1),
             )
 
-        for g in range(G - 1):
+        kaccs = [bank("kacc%d" % j) for j in range(4)]
+        for g in range(G):
+            wt = load(1, k_w_words, 0, g)
+            for j in range(4):
+                x_pass(kaccs, 1, g, j, wt, BANK * j)
+        kres = rpool.tile([P, ROUND], F32, tag="res", name="kres")
+        for half in range(2):
+            tmp = tpool.tile([P, 2 * BANK], F32, tag="tmp", name="ktmp%d" % half)
+            for jj in range(2):
+                c = 2 * half + jj
+                acc = kaccs[c][:].rearrange("p (h d) -> p h d", d=HD)
+                nc.vector.tensor_tensor(
+                    out=kres[:, BANK * c:BANK * (c + 1)].rearrange("p (h d) -> p h d", d=HD), in0=acc,
+                    in1=cos_f[:].unsqueeze(1).to_broadcast([P, 4, HD]), op=MULT)
+                nc.vector.tensor_tensor(
+                    out=tmp[:, BANK * jj:BANK * (jj + 1)].rearrange("p (h d) -> p h d", d=HD), in0=acc,
+                    in1=swp_f[:].unsqueeze(1).to_broadcast([P, 4, HD]), op=MULT)
+            res4 = kres[:, 2 * BANK * half:2 * BANK * (half + 1)].rearrange("p (n w d) -> p n w d", w=2, d=64)
+            tmp4 = tmp[:].rearrange("p (n w d) -> p n w d", w=2, d=64)
+            for w in range(2):
+                nc.vector.tensor_tensor(out=res4[:, :, w, :], in0=res4[:, :, w, :], in1=tmp4[:, :, 1 - w, :], op=ADD)
+            for b in range(B):
+                nc.gpsimd.dma_start(
+                    out=out_1[b, 8 * half:8 * (half + 1)].rearrange("h s d -> s h d"),
+                    in_=kres[b:P:2, 2 * BANK * half:2 * BANK * (half + 1)].rearrange("p (h d) -> p h d", d=HD),
+                )
+
+        accs = [bank("acc%d" % j) for j in range(4)]
+        for g in range(G - 2):
             wt = load(2, v_w_words, 0, g)
             for j in range(4):
-                v_pass(g, j, wt, BANK * j)
-        flat = v_w_words[G - 1].rearrange("p n t -> p (n t)")
+                x_pass(accs, 2, g, j, wt, BANK * j)
         for j in range(4):
-            wl = wlast.tile([P, BANK], U32, align_bytes=64, tag="wl", name="wl%d" % j)
-            nc.sync.dma_start(out=wl[:].bitcast(I32), in_=flat[:, 4 * BANK * j:4 * BANK * (j + 1)].bitcast(I32))
-            v_pass(G - 1, j, wl, 0)
+            for g in (G - 2, G - 1):
+                wl = wlast.tile([P, BANK], U32, align_bytes=64, tag="wl", name="wl%d_%d" % (g, j))
+                flat = v_w_words[g].rearrange("p n t -> p (n t)")
+                nc.sync.dma_start(out=wl[:].bitcast(I32), in_=flat[:, 4 * BANK * j:4 * BANK * (j + 1)].bitcast(I32))
+                x_pass(accs, 2, g, j, wl, 0)
         for j in range(4):
             vres = vpool.tile([P, BANK], F32, tag="vres", name="vres%d" % j)
-            if j % 2 == 0:
-                nc.vector.tensor_copy(out=vres[:], in_=accs[j][:])
-            else:
-                nc.scalar.copy(out=vres[:], in_=accs[j][:])
+            nc.scalar.copy(out=vres[:], in_=accs[j][:])
             for b in range(B):
-                eng = nc.sync if b == 0 else nc.scalar
-                eng.dma_start(
+                nc.sync.dma_start(
                     out=out_2[b, 4 * j:4 * j + 4].rearrange("h s d -> s h d"),
                     in_=vres[b:P:2, :].rearrange("p (h d) -> p h d", d=HD),
                 )

@@ -18,7 +18,6 @@ G = H // 512
 NQ, NKV = 4096, 2048
 BANK = 512
 ROUND = 2048
-SP, SI = 4, 16
 PB_OFF = (0, 8, 8)
 FLOPS = 2 * B * S * H * (NQ + 2 * NKV)
 
@@ -33,7 +32,6 @@ def tile_mistralattention_w_kernel(
         const = ctx.enter_context(tc.tile_pool(name="const", bufs=1))
         wpool = ctx.enter_context(tc.tile_pool(name="wpool", bufs=13))
         wlast = ctx.enter_context(tc.tile_pool(name="wlast", bufs=8))
-        zpool = ctx.enter_context(tc.tile_pool(name="zpool", bufs=2))
         rpool = ctx.enter_context(tc.tile_pool(name="rpool", bufs=2))
         tpool = ctx.enter_context(tc.tile_pool(name="tpool", bufs=2))
         vpool = ctx.enter_context(tc.tile_pool(name="vpool", bufs=4))
@@ -53,14 +51,6 @@ def tile_mistralattention_w_kernel(
 
         x_sb = const.tile([P, H], BF16, align_bytes=64)
         nc.sync.dma_start(out=x_sb[:], in_=hidden_states.rearrange("b s k -> (b s) k"))
-
-        cosr = zpool.tile([P, SI * HD], BF16, tag="zt", name="cosr")
-        sinr = zpool.tile([P, SI * HD], BF16, tag="zt", name="sinr")
-        nc.vector.memset(cosr[:].bitcast(I32), 0)
-        nc.vector.memset(sinr[:].bitcast(I32), 0)
-        for b in range(B):
-            nc.scalar.dma_start(out=cosr[b:2 * SP:2, :], in_=cos[b].rearrange("(sp si) d -> sp (si d)", sp=SP))
-            nc.scalar.dma_start(out=sinr[b:2 * SP:2, :], in_=sin[b].rearrange("(sp si) d -> sp (si d)", sp=SP))
 
         cos_bf = const.tile([P, HD], BF16)
         sin_bf = const.tile([P, HD], BF16)
@@ -85,21 +75,13 @@ def tile_mistralattention_w_kernel(
                 )
 
         perm_v = const.tile([P, P], F32)
-        perm_t = const.tile([P, P], F32)
         nc.vector.tensor_copy(
             out=perm_v[:].rearrange("p (s b) -> p s b", b=B),
             in_=ident[:].rearrange("p (b s) -> p s b", b=B))
-        nc.vector.tensor_copy(
-            out=perm_t[:].rearrange("p (sp b si) -> p sp b si", sp=SP, b=B),
-            in_=ident[:].rearrange("p (b sp si) -> p sp b si", sp=SP, b=B))
-        sel = const.tile([P, P], BF16)
-        nc.vector.tensor_copy(
-            out=sel[:].rearrange("p (h e) -> p h e", e=8),
-            in_=ident[:, 0:8].unsqueeze(1).to_broadcast([P, 16, 8]))
 
         xw = x_sb[:].bitcast(F32)
         codes = []
-        for which, perm in ((0, perm_t), (1, perm_v)):
+        for which, perm in ((1, perm_v),):
             grouped = const.tile([P, G, P, 4], BF16, align_bytes=64, name="grouped%d" % which)
             grouped_w = grouped[:].bitcast(F32)
             x_codes = const.tile([P, G * P], U32, align_bytes=64, name="x_codes%d" % which)
@@ -128,24 +110,7 @@ def tile_mistralattention_w_kernel(
                     in_=grouped[:, 2 * j:2 * j + 2, :, :].rearrange("p g m t -> p (g m t)"),
                 )
             codes.append((x_codes, x_scales))
-        xt_codes, xt_scales = codes[0]
-        xv_codes, xv_scales = codes[1]
-
-        ssr = rpool.tile([P, SI * HD], BF16, tag="res", name="ssr")
-        sin3 = sinr[:].rearrange("p (si w d) -> p si w d", w=2, d=64)
-        ssr3 = ssr[:].rearrange("p (si w d) -> p si w d", w=2, d=64)
-        nc.vector.tensor_copy(out=ssr3[:, :, 0, :], in_=sin3[:, :, 1, :])
-        nc.vector.tensor_scalar(out=ssr3[:, :, 1, :], in0=sin3[:, :, 0, :], scalar1=-1.0, scalar2=None, op0=MULT)
-        cos_t = const.tile([P, SI * HD], F32)
-        swp_t = const.tile([P, SI * HD], F32)
-        for which, (rows, table) in enumerate(((cosr, cos_t), (ssr, swp_t))):
-            for c in range(4):
-                tb = bank("tb%d_%d" % (which, c))
-                nc.tensor.matmul(out=tb[:], lhsT=sel[:], rhs=rows[:, BANK * c:BANK * (c + 1)], start=True, stop=True)
-                if c % 2 == 0:
-                    nc.scalar.copy(out=table[:, BANK * c:BANK * (c + 1)], in_=tb[:])
-                else:
-                    nc.vector.tensor_copy(out=table[:, BANK * c:BANK * (c + 1)], in_=tb[:])
+        xv_codes, xv_scales = codes[0]
 
         cos_f = const.tile([P, HD], F32)
         swp_f = const.tile([P, HD], F32)
@@ -165,109 +130,61 @@ def tile_mistralattention_w_kernel(
             nc.sync.dma_start(out=wt[:].bitcast(I32), in_=flat[:, 4 * c0:4 * (c0 + ROUND)].bitcast(I32))
             return wt
 
-        def rotary_round(kind, words, c0, out, h0, cuts):
-            label = "%d_%d" % (kind, c0)
-            wts = [load(kind, words, c0, g) for g in range(G)]
-            yts = [bank("yt%s_%d" % (label, bk)) for bk in range(4)]
-
-            def one_pass(bk, slot, g):
-                col = HD * (4 * bk + slot)
-                nc.tensor.matmul_mx(
-                    out=yts[bk][:, HD * slot:HD * (slot + 1)],
-                    lhsT=wts[g][:, col:col + HD].bitcast(FP8X4),
-                    lhsT_scale=plane(kind, g, c0 + col, HD),
-                    rhs=xt_codes[:, P * g:P * (g + 1)].bitcast(FP8X4),
-                    rhs_scale=xt_scales[:, P * g:P * (g + 1)],
-                    start=(g == 0),
-                    stop=(g == G - 1),
-                )
-
-            for g in range(G):
-                for bk in range(4):
-                    one_pass(bk, 0, g)
-            zt = zpool.tile([P, SI, P], F32, tag="zt", name="zt%s" % label)
-            for bk in range(4):
-                for slot in range(1, 4):
-                    for g in range(G):
-                        one_pass(bk, slot, g)
-                nc.scalar.copy(
-                    out=zt[:, :, 32 * bk:32 * (bk + 1)],
-                    in_=yts[bk][:].rearrange("p (he si) -> p si he", si=SI))
-            fs = [bank("f%s_%d" % (label, c)) for c in range(4)]
-            for si in range(SI):
-                nc.tensor.transpose(fs[si // 4][:, HD * (si % 4):HD * (si % 4 + 1)], zt[:, si, :], ident[:])
-            res = rpool.tile([P, ROUND], F32, tag="res", name="res%s" % label)
-            for half in range(2):
-                tmp = tpool.tile([P, 2 * BANK], F32, tag="tmp", name="tmp%s_%d" % (label, half))
-                for jj in range(2):
-                    c = 2 * half + jj
-                    cols = slice(BANK * c, BANK * (c + 1))
-                    nc.vector.tensor_tensor(out=res[:, cols], in0=fs[c][:], in1=cos_t[:, cols], op=MULT)
-                    nc.vector.tensor_tensor(out=tmp[:, BANK * jj:BANK * (jj + 1)], in0=fs[c][:], in1=swp_t[:, cols], op=MULT)
-                res4 = res[:, 2 * BANK * half:2 * BANK * (half + 1)].rearrange("p (n w d) -> p n w d", w=2, d=64)
-                tmp4 = tmp[:].rearrange("p (n w d) -> p n w d", w=2, d=64)
-                for w in range(2):
-                    nc.vector.tensor_tensor(out=res4[:, :, w, :], in0=res4[:, :, w, :], in1=tmp4[:, :, 1 - w, :], op=ADD)
-                if cuts == 2 or half == 1:
-                    lo = 2 * BANK * half if cuts == 2 else 0
-                    for b in range(B):
-                        nc.gpsimd.dma_start(
-                            out=out[b, h0:h0 + 16].rearrange("h (sp si) d -> (h sp) (si d)", sp=SP)[:, lo:2 * BANK * (half + 1)],
-                            in_=res[b:P:2, lo:2 * BANK * (half + 1)],
-                        )
-
-        rotary_round(0, q_w_words, 0, out_0, 0, 1)
-        rotary_round(0, q_w_words, ROUND, out_0, 16, 1)
-
-        def x_pass(accs, kind, g, j, wt, lo):
+        def x_pass(accs, kind, g, j, wt, lo, c0):
             nc.tensor.matmul_mx(
                 out=accs[j][:],
                 lhsT=xv_codes[:, P * g:P * (g + 1)].bitcast(FP8X4),
                 lhsT_scale=xv_scales[:, P * g:P * (g + 1)],
                 rhs=wt[:, lo:lo + BANK].bitcast(FP8X4),
-                rhs_scale=plane(kind, g, BANK * j, BANK),
+                rhs_scale=plane(kind, g, c0 + BANK * j, BANK),
                 start=(g == 0),
                 stop=(g == G - 1),
             )
 
-        kaccs = [bank("kacc%d" % j) for j in range(4)]
-        for g in range(G):
-            wt = load(1, k_w_words, 0, g)
-            for j in range(4):
-                x_pass(kaccs, 1, g, j, wt, BANK * j)
-        kres = rpool.tile([P, ROUND], F32, tag="res", name="kres")
-        for half in range(2):
-            tmp = tpool.tile([P, 2 * BANK], F32, tag="tmp", name="ktmp%d" % half)
-            for jj in range(2):
-                c = 2 * half + jj
-                acc = kaccs[c][:].rearrange("p (h d) -> p h d", d=HD)
-                nc.vector.tensor_tensor(
-                    out=kres[:, BANK * c:BANK * (c + 1)].rearrange("p (h d) -> p h d", d=HD), in0=acc,
-                    in1=cos_f[:].unsqueeze(1).to_broadcast([P, 4, HD]), op=MULT)
-                nc.vector.tensor_tensor(
-                    out=tmp[:, BANK * jj:BANK * (jj + 1)].rearrange("p (h d) -> p h d", d=HD), in0=acc,
-                    in1=swp_f[:].unsqueeze(1).to_broadcast([P, 4, HD]), op=MULT)
-            res4 = kres[:, 2 * BANK * half:2 * BANK * (half + 1)].rearrange("p (n w d) -> p n w d", w=2, d=64)
-            tmp4 = tmp[:].rearrange("p (n w d) -> p n w d", w=2, d=64)
-            for w in range(2):
-                nc.vector.tensor_tensor(out=res4[:, :, w, :], in0=res4[:, :, w, :], in1=tmp4[:, :, 1 - w, :], op=ADD)
-            for b in range(B):
-                nc.gpsimd.dma_start(
-                    out=out_1[b, 8 * half:8 * (half + 1)].rearrange("h s d -> s h d"),
-                    in_=kres[b:P:2, 2 * BANK * half:2 * BANK * (half + 1)].rearrange("p (h d) -> p h d", d=HD),
-                )
+        def rotary_round(kind, words, c0, out, h0):
+            label = "%d_%d" % (kind, c0)
+            kaccs = [bank("kacc%s_%d" % (label, j)) for j in range(4)]
+            for g in range(G):
+                wt = load(kind, words, c0, g)
+                for j in range(4):
+                    x_pass(kaccs, kind, g, j, wt, BANK * j, c0)
+            kres = rpool.tile([P, ROUND], F32, tag="res", name="kres%s" % label)
+            for half in range(2):
+                tmp = tpool.tile([P, 2 * BANK], F32, tag="tmp", name="ktmp%s_%d" % (label, half))
+                for jj in range(2):
+                    c = 2 * half + jj
+                    acc = kaccs[c][:].rearrange("p (h d) -> p h d", d=HD)
+                    nc.vector.tensor_tensor(
+                        out=kres[:, BANK * c:BANK * (c + 1)].rearrange("p (h d) -> p h d", d=HD), in0=acc,
+                        in1=cos_f[:].unsqueeze(1).to_broadcast([P, 4, HD]), op=MULT)
+                    nc.vector.tensor_tensor(
+                        out=tmp[:, BANK * jj:BANK * (jj + 1)].rearrange("p (h d) -> p h d", d=HD), in0=acc,
+                        in1=swp_f[:].unsqueeze(1).to_broadcast([P, 4, HD]), op=MULT)
+                res4 = kres[:, 2 * BANK * half:2 * BANK * (half + 1)].rearrange("p (n w d) -> p n w d", w=2, d=64)
+                tmp4 = tmp[:].rearrange("p (n w d) -> p n w d", w=2, d=64)
+                for w in range(2):
+                    nc.vector.tensor_tensor(out=res4[:, :, w, :], in0=res4[:, :, w, :], in1=tmp4[:, :, 1 - w, :], op=ADD)
+                for b in range(B):
+                    nc.gpsimd.dma_start(
+                        out=out[b, h0 + 8 * half:h0 + 8 * (half + 1)].rearrange("h s d -> s h d"),
+                        in_=kres[b:P:2, 2 * BANK * half:2 * BANK * (half + 1)].rearrange("p (h d) -> p h d", d=HD),
+                    )
+
+        rotary_round(0, q_w_words, 0, out_0, 0)
+        rotary_round(0, q_w_words, ROUND, out_0, 16)
+        rotary_round(1, k_w_words, 0, out_1, 0)
 
         accs = [bank("acc%d" % j) for j in range(4)]
         for g in range(G - 2):
             wt = load(2, v_w_words, 0, g)
             for j in range(4):
-                x_pass(accs, 2, g, j, wt, BANK * j)
+                x_pass(accs, 2, g, j, wt, BANK * j, 0)
         for j in range(4):
             for g in (G - 2, G - 1):
                 wl = wlast.tile([P, BANK], U32, align_bytes=64, tag="wl", name="wl%d_%d" % (g, j))
                 flat = v_w_words[g].rearrange("p n t -> p (n t)")
                 nc.sync.dma_start(out=wl[:].bitcast(I32), in_=flat[:, 4 * BANK * j:4 * BANK * (j + 1)].bitcast(I32))
-                x_pass(accs, 2, g, j, wl, 0)
+                x_pass(accs, 2, g, j, wl, 0, 0)
         for j in range(4):
             vres = vpool.tile([P, BANK], F32, tag="vres", name="vres%d" % j)
             nc.scalar.copy(out=vres[:], in_=accs[j][:])

@@ -32,7 +32,7 @@ def tile_mistralattention_w_kernel(
         const = ctx.enter_context(tc.tile_pool(name="const", bufs=1))
         wpool = ctx.enter_context(tc.tile_pool(name="wpool", bufs=13))
         wlast = ctx.enter_context(tc.tile_pool(name="wlast", bufs=8))
-        rpool = ctx.enter_context(tc.tile_pool(name="rpool", bufs=2))
+        rpool = ctx.enter_context(tc.tile_pool(name="rpool", bufs=3))
         tpool = ctx.enter_context(tc.tile_pool(name="tpool", bufs=2))
         vpool = ctx.enter_context(tc.tile_pool(name="vpool", bufs=4))
         psum = ctx.enter_context(tc.psum_pool(name="psum", bufs=8))
@@ -141,6 +141,8 @@ def tile_mistralattention_w_kernel(
                 stop=(g == G - 1),
             )
 
+        late_stores = []
+
         def rotary_round(kind, words, c0, out, h0):
             label = "%d_%d" % (kind, c0)
             kaccs = [bank("kacc%s_%d" % (label, j)) for j in range(4)]
@@ -165,10 +167,10 @@ def tile_mistralattention_w_kernel(
                 for w in range(2):
                     nc.vector.tensor_tensor(out=res4[:, :, w, :], in0=res4[:, :, w, :], in1=tmp4[:, :, 1 - w, :], op=ADD)
                 for b in range(B):
-                    nc.gpsimd.dma_start(
-                        out=out[b, h0 + 8 * half:h0 + 8 * (half + 1)].rearrange("h s d -> s h d"),
-                        in_=kres[b:P:2, 2 * BANK * half:2 * BANK * (half + 1)].rearrange("p (h d) -> p h d", d=HD),
-                    )
+                    late_stores.append((
+                        out[b, h0 + 8 * half:h0 + 8 * (half + 1)].rearrange("h s d -> s h d"),
+                        kres[b:P:2, 2 * BANK * half:2 * BANK * (half + 1)].rearrange("p (h d) -> p h d", d=HD),
+                    ))
 
         rotary_round(0, q_w_words, 0, out_0, 0)
         rotary_round(0, q_w_words, ROUND, out_0, 16)
@@ -185,6 +187,8 @@ def tile_mistralattention_w_kernel(
                 flat = v_w_words[g].rearrange("p n t -> p (n t)")
                 nc.sync.dma_start(out=wl[:].bitcast(I32), in_=flat[:, 4 * BANK * j:4 * BANK * (j + 1)].bitcast(I32))
                 x_pass(accs, 2, g, j, wl, 0, 0)
+        for dst, res in late_stores:
+            nc.sync.dma_start(out=dst, in_=res)
         for j in range(4):
             vres = vpool.tile([P, BANK], F32, tag="vres", name="vres%d" % j)
             nc.scalar.copy(out=vres[:], in_=accs[j][:])

@@ -19,6 +19,8 @@ NQ, NKV = 4096, 2048
 BANK = 512
 ROUND = 2048
 PB_OFF = (0, 8, 8)
+PA_ORDER = ((0, 1, 2, 3), (2, 3, 0, 1), (0, 1, 2, 3))
+PB_ORDER = ((0, 2, 1, 3), (0, 2, 1, 3), (2, 0, 3, 1))
 FLOPS = 2 * B * S * H * (NQ + 2 * NKV)
 
 
@@ -63,12 +65,12 @@ def tile_mistralattention_w_kernel(
 
         for kind, scl in enumerate((q_w_scales, k_w_scales, v_w_scales)):
             pa, pb = planes[kind]
-            for quad in (0, 2, 1, 3):
+            for quad in PA_ORDER[kind]:
                 nc.gpsimd.dma_start(
                     out=pa[32 * quad:32 * quad + 16, :].bitcast(F32),
                     in_=scl[0:4, 4 * quad:4 * quad + 4, :].bitcast(F32),
                 )
-            for quad in (0, 2, 1, 3):
+            for quad in PB_ORDER[kind]:
                 nc.gpsimd.dma_start(
                     out=pb[32 * quad + PB_OFF[kind]:32 * quad + PB_OFF[kind] + 8, :].bitcast(F32),
                     in_=scl[4:6, 4 * quad:4 * quad + 4, :].bitcast(F32),

from contextlib import ExitStack

import concourse.mybir as mybir
from concourse.masks import make_identity

F32 = mybir.dt.float32
BF16 = mybir.dt.bfloat16
I32 = mybir.dt.int32
U32 = mybir.dt.uint32
U8 = mybir.dt.uint8
FP8X4 = mybir.dt.float8_e4m3fn_x4
MULT = mybir.AluOpType.mult
ADD = mybir.AluOpType.add

P = 128
B, S, H, HD = 2, 64, 3072, 128
G = H // 512
NQ, NKV = 4096, 2048
BANK = 512
ROUND = 2048
PB_OFF = (0, 8, 8)
PA_ORDER = ((0, 1, 2, 3), (2, 3, 0, 1), (0, 1, 2, 3))
PB_ORDER = ((0, 2, 1, 3), (0, 2, 1, 3), (2, 0, 3, 1))
FLOPS = 2 * B * S * H * (NQ + 2 * NKV)


def tile_mistralattention_w_kernel(
    tc, hidden_states, cos, sin,
    q_w_words, q_w_scales, k_w_words, k_w_scales, v_w_words, v_w_scales,
    out_0, out_1, out_2,
):
    nc = tc.nc
    with ExitStack() as ctx:
        const = ctx.enter_context(tc.tile_pool(name="const", bufs=1))
        wpool = ctx.enter_context(tc.tile_pool(name="wpool", bufs=13))
        wlast = ctx.enter_context(tc.tile_pool(name="wlast", bufs=8))
        rpool = ctx.enter_context(tc.tile_pool(name="rpool", bufs=3))
        tpool = ctx.enter_context(tc.tile_pool(name="tpool", bufs=2))
        vpool = ctx.enter_context(tc.tile_pool(name="vpool", bufs=4))
        psum = ctx.enter_context(tc.psum_pool(name="psum", bufs=8))
        ctx.enter_context(tc.manual_schedule())

        def bank(name):
            return psum.tile([P, BANK], F32, tag="bank", name=name)

        planes = []
        for kind, n in enumerate((NQ, NKV, NKV)):
            pa = const.tile([P, n], U8, align_bytes=64, name="pa%d" % kind)
            pb = const.tile([P, n], U8, align_bytes=64, name="pb%d" % kind)
            nc.vector.memset(pa[:].bitcast(I32), 0)
            nc.vector.memset(pb[:].bitcast(I32), 0)
            planes.append((pa, pb))

        x_sb = const.tile([P, H], BF16, align_bytes=64)
        nc.sync.dma_start(out=x_sb[:], in_=hidden_states.rearrange("b s k -> (b s) k"))

        cos_bf = const.tile([P, HD], BF16)
        sin_bf = const.tile([P, HD], BF16)
        for b in range(B):
            nc.scalar.dma_start(out=cos_bf[b:P:2, :], in_=cos[b])
            nc.scalar.dma_start(out=sin_bf[b:P:2, :], in_=sin[b])

        ident = const.tile([P, P], F32)
        make_identity(nc, ident[:])

        for kind, scl in enumerate((q_w_scales, k_w_scales, v_w_scales)):
            pa, pb = planes[kind]
            for quad in PA_ORDER[kind]:
                nc.gpsimd.dma_start(
                    out=pa[32 * quad:32 * quad + 16, :].bitcast(F32),
                    in_=scl[0:4, 4 * quad:4 * quad + 4, :].bitcast(F32),
                )
            for quad in PB_ORDER[kind]:
                nc.gpsimd.dma_start(
                    out=pb[32 * quad + PB_OFF[kind]:32 * quad + PB_OFF[kind] + 8, :].bitcast(F32),
                    in_=scl[4:6, 4 * quad:4 * quad + 4, :].bitcast(F32),
                )

        perm_v = const.tile([P, P], F32)
        nc.vector.tensor_copy(
            out=perm_v[:].rearrange("p (s b) -> p s b", b=B),
            in_=ident[:].rearrange("p (b s) -> p s b", b=B))

        xw = x_sb[:].bitcast(F32)
        codes = []
        for which, perm in ((1, perm_v),):
            grouped = const.tile([P, G, P, 4], BF16, align_bytes=64, name="grouped%d" % which)
            grouped_w = grouped[:].bitcast(F32)
            x_codes = const.tile([P, G * P], U32, align_bytes=64, name="x_codes%d" % which)
            x_scales = const.tile([P, G * P], U8, align_bytes=64, name="x_scales%d" % which)
            xts = []
            for j in range(G // 2):
                xt = bank("xt%d_%d" % (which, j))
                for gi in range(2):
                    g = 2 * j + gi
                    for u in range(2):
                        nc.tensor.transpose(
                            xt[:, 128 * (2 * gi + u):128 * (2 * gi + u + 1)],
                            xw[:, 256 * g + u:256 * (g + 1):2], perm[:])
                xts.append(xt)
            for j in range(G // 2):
                src = xts[j][:].rearrange("p (g u m) -> p g m u", g=2, u=2)
                dst = grouped_w[:, 2 * j:2 * j + 2, :, :]
                if j == 1:
                    nc.scalar.copy(out=dst, in_=src)
                else:
                    nc.vector.tensor_copy(out=dst, in_=src)
            for j in range(G // 2):
                nc.vector.quantize_mx(
                    out=x_codes[:, 256 * j:256 * (j + 1)].bitcast(FP8X4),
                    scales=x_scales[:, 256 * j:256 * (j + 1)],
                    in_=grouped[:, 2 * j:2 * j + 2, :, :].rearrange("p g m t -> p (g m t)"),
                )
            codes.append((x_codes, x_scales))
        xv_codes, xv_scales = codes[0]

        cos_f = const.tile([P, HD], F32)
        swp_f = const.tile([P, HD], F32)
        nc.vector.tensor_copy(out=cos_f[:], in_=cos_bf[:])
        nc.vector.tensor_copy(out=swp_f[:, 0:64], in_=sin_bf[:, 64:128])
        nc.vector.tensor_scalar(out=swp_f[:, 64:128], in0=sin_bf[:, 0:64], scalar1=-1.0, scalar2=None, op0=MULT)

        def plane(kind, g, c0, n):
            pa, pb = planes[kind]
            if g < 4:
                return pa[4 * g:P, c0:c0 + n]
            return pb[PB_OFF[kind] + 4 * (g - 4):P, c0:c0 + n]

        def load(kind, words, c0, g):
            wt = wpool.tile([P, ROUND], U32, align_bytes=64, tag="wt", name="wt%d_%d_%d" % (kind, c0, g))
            flat = words[g].rearrange("p n t -> p (n t)")
            nc.sync.dma_start(out=wt[:].bitcast(I32), in_=flat[:, 4 * c0:4 * (c0 + ROUND)].bitcast(I32))
            return wt

        def x_pass(accs, kind, g, j, wt, lo, c0):
            nc.tensor.matmul_mx(
                out=accs[j][:],
                lhsT=xv_codes[:, P * g:P * (g + 1)].bitcast(FP8X4),
                lhsT_scale=xv_scales[:, P * g:P * (g + 1)],
                rhs=wt[:, lo:lo + BANK].bitcast(FP8X4),
                rhs_scale=plane(kind, g, c0 + BANK * j, BANK),
                start=(g == 0),
                stop=(g == G - 1),
            )

        late_stores = []

        def rotary_round(kind, words, c0, out, h0):
            label = "%d_%d" % (kind, c0)
            kaccs = [bank("kacc%s_%d" % (label, j)) for j in range(4)]
            for g in range(G):
                wt = load(kind, words, c0, g)
                for j in range(4):
                    x_pass(kaccs, kind, g, j, wt, BANK * j, c0)
            kres = rpool.tile([P, ROUND], F32, tag="res", name="kres%s" % label)
            for half in range(2):
                tmp = tpool.tile([P, 2 * BANK], F32, tag="tmp", name="ktmp%s_%d" % (label, half))
                for jj in range(2):
                    c = 2 * half + jj
                    acc = kaccs[c][:].rearrange("p (h d) -> p h d", d=HD)
                    nc.vector.tensor_tensor(
                        out=kres[:, BANK * c:BANK * (c + 1)].rearrange("p (h d) -> p h d", d=HD), in0=acc,
                        in1=cos_f[:].unsqueeze(1).to_broadcast([P, 4, HD]), op=MULT)
                    nc.vector.tensor_tensor(
                        out=tmp[:, BANK * jj:BANK * (jj + 1)].rearrange("p (h d) -> p h d", d=HD), in0=acc,
                        in1=swp_f[:].unsqueeze(1).to_broadcast([P, 4, HD]), op=MULT)
                res4 = kres[:, 2 * BANK * half:2 * BANK * (half + 1)].rearrange("p (n w d) -> p n w d", w=2, d=64)
                tmp4 = tmp[:].rearrange("p (n w d) -> p n w d", w=2, d=64)
                for w in range(2):
                    nc.vector.tensor_tensor(out=res4[:, :, w, :], in0=res4[:, :, w, :], in1=tmp4[:, :, 1 - w, :], op=ADD)
                for b in range(B):
                    late_stores.append((
                        out[b, h0 + 8 * half:h0 + 8 * (half + 1)].rearrange("h s d -> s h d"),
                        kres[b:P:2, 2 * BANK * half:2 * BANK * (half + 1)].rearrange("p (h d) -> p h d", d=HD),
                    ))

        rotary_round(0, q_w_words, 0, out_0, 0)
        rotary_round(0, q_w_words, ROUND, out_0, 16)
        rotary_round(1, k_w_words, 0, out_1, 0)

        accs = [bank("acc%d" % j) for j in range(4)]
        for g in range(G - 2):
            wt = load(2, v_w_words, 0, g)
            for j in range(4):
                x_pass(accs, 2, g, j, wt, BANK * j, 0)
        for j in range(4):
            for g in (G - 2, G - 1):
                wl = wlast.tile([P, BANK], U32, align_bytes=64, tag="wl", name="wl%d_%d" % (g, j))
                flat = v_w_words[g].rearrange("p n t -> p (n t)")
                nc.sync.dma_start(out=wl[:].bitcast(I32), in_=flat[:, 4 * BANK * j:4 * BANK * (j + 1)].bitcast(I32))
                x_pass(accs, 2, g, j, wl, 0, 0)
        for dst, res in late_stores:
            nc.sync.dma_start(out=dst, in_=res)
        for j in range(4):
            vres = vpool.tile([P, BANK], F32, tag="vres", name="vres%d" % j)
            nc.scalar.copy(out=vres[:], in_=accs[j][:])
            for b in range(B):
                nc.sync.dma_start(
                    out=out_2[b, 4 * j:4 * j + 4].rearrange("h s d -> s h d"),
                    in_=vres[b:P:2, :].rearrange("p (h d) -> p h d", d=HD),
                )
